import numpy as np
import ml_dtypes


def mxq(x, axis, fmt="e4m3"):
    dtype, down = {"e4m3": (ml_dtypes.float8_e4m3fn, 7), "e5m2": (ml_dtypes.float8_e5m2, 14)}[fmt]
    v = np.moveaxis(np.asarray(x, np.float32).astype(ml_dtypes.bfloat16).astype(np.float64), axis, -1)
    blocks = v.reshape(v.shape[:-1] + (-1, 32))
    amax = np.abs(blocks).max(-1, keepdims=True)
    byte = np.maximum(np.where(amax > 0, np.frexp(amax)[1] - 1 + 127, 0) - down, 1)
    scale = np.exp2(byte - 127.0)
    codes = (blocks / scale).astype(np.float32).astype(dtype).astype(np.float64)
    return np.moveaxis((codes * scale).reshape(v.shape), -1, axis)


WIDE = False


def mx_kscale(k):
    if not WIDE:
        return np.ones(k)
    levels = np.array([10, -10, 5, -5, 0])
    if k % 512:
        return np.exp2(np.random.permutation(np.resize(levels, k // 32))).repeat(32)
    a = np.empty((k // 512, 16))
    for p in range(k // 512):
        a[p, :8] = np.random.permutation(np.resize(levels, 8))
        for g in range(8):
            far = levels[np.abs(levels - a[p, g]) >= 10]
            a[p, g + 8] = far[np.random.randint(len(far))]
    return np.exp2(a.ravel()).repeat(32)


BF16 = ml_dtypes.bfloat16


def bf(x):
    return np.asarray(x, np.float32).astype(BF16)


def f64(x):
    return np.asarray(x).astype(np.float64)


B, S, D, E = 2, 2048, 512, 256
EPS = 1e-5


def layer_norm(x, g, b):
    mu = x.mean(-1, keepdims=True)
    var = np.square(x - mu).mean(-1, keepdims=True)
    return (x - mu) / np.sqrt(var + EPS) * g + b


def setup_inputs():
    s = mx_kscale(D)

    def stream():
        return bf(np.random.standard_normal((B, S, D)) + 0.5 * np.random.standard_normal((B, S, 1)))

    def gain():
        return bf((1.0 + 0.1 * np.random.standard_normal(D)) * s)

    def shift():
        return bf(0.1 * np.random.standard_normal(D) * s)

    def weight(a):
        return bf(np.random.standard_normal((E, D)) * a / np.sqrt(D) / s[None, :])

    def bias():
        return bf(0.2 * np.random.standard_normal(E))

    return {"text": stream(), "img": stream(),
            "ln_t_g": gain(), "ln_t_b": shift(), "ln_i_g": gain(), "ln_i_b": shift(),
            "Wq": weight(1.5), "bq": bias(),
            "Wkt": weight(1.5), "bkt": bias(), "Wvt": weight(1.0), "bvt": bias(),
            "Wki": weight(1.5), "bki": bias(), "Wvi": weight(1.0), "bvi": bias()}


def reference(text, img, ln_t_g, ln_t_b, ln_i_g, ln_i_b, Wq, bq, Wkt, bkt, Wvt, bvt, Wki, bki, Wvi, bvi):
    tn = mxq(layer_norm(f64(text), f64(ln_t_g), f64(ln_t_b)), 2, "e4m3")
    im = mxq(layer_norm(f64(img), f64(ln_i_g), f64(ln_i_b)), 2, "e4m3")
    wq = mxq(f64(Wq), 1, "e4m3").T
    q = np.concatenate([(tn @ wq), (im @ wq)], 0) + f64(bq)
    k = np.concatenate([(tn @ mxq(f64(Wkt), 1, "e4m3").T) + f64(bkt), (im @ mxq(f64(Wki), 1, "e4m3").T) + f64(bki)], 0)
    v = np.concatenate([(tn @ mxq(f64(Wvt), 1, "e4m3").T) + f64(bvt), (im @ mxq(f64(Wvi), 1, "e4m3").T) + f64(bvi)], 0)
    return q, k, v

@@ -1,0 +1,284 @@
+from contextlib import ExitStack
+
+import concourse.mybir as mybir
+from concourse.masks import make_identity
+
+F32 = mybir.dt.float32
+BF16 = mybir.dt.bfloat16
+U32 = mybir.dt.uint32
+U8 = mybir.dt.uint8
+FP8X4 = mybir.dt.float8_e4m3fn_x4
+ACT = mybir.ActivationFunctionType
+ALU = mybir.AluOpType
+
+P = 128
+PACK = 4
+D = P * PACK
+E = 256
+SLOTS = 4
+GROUP = P * SLOTS
+TOKENS = 4096
+GROUPS_PER_STREAM = TOKENS // GROUP
+N_GROUPS = 2 * GROUPS_PER_STREAM
+N_WEIGHTS = 5
+BANK = 512
+EPS = 1e-5
+
+FLOPS = 2 * (2 * TOKENS) * D * (3 * E)
+
+FIRST_LOADS = 2
+LAG_SCALARS = 1
+LAG_NORMALISE = 2
+LAG_TRANSPOSE = 3
+LAG_PROJECT = 5
+
+
+def tile_modalityadaptivemodule_pa_t_kernel(
+    tc,
+    text, img, ln_t_g, ln_t_b, ln_i_g, ln_i_b,
+    Wq, bq, Wkt, bkt, Wvt, bvt, Wki, bki, Wvi, bvi,
+    out_0, out_1, out_2,
+):
+    nc = tc.nc
+    weights = [Wq, Wkt, Wvt, Wki, Wvi]
+    biases = [bq, bkt, bvt, bki, bvi]
+    ln_vectors = [ln_t_g, ln_t_b, ln_i_g, ln_i_b]
+
+    def weight_columns(g, o):
+        w = 0 if o == 0 else o + 2 * (g // GROUPS_PER_STREAM)
+        return slice(w * E, (w + 1) * E)
+
+    x_groups = [
+        s.flatten_outer_dims().rearrange("(g p j) d -> g p (j d)", p=P, j=SLOTS) for s in (text, img)
+    ]
+    out_groups = [
+        o.flatten_outer_dims().rearrange("(g p j) e -> g p (j e)", p=P, j=SLOTS)
+        for o in (out_0, out_1, out_2)
+    ]
+
+    with ExitStack() as stack:
+        const = stack.enter_context(tc.tile_pool(name="const", bufs=1))
+        wprep = stack.enter_context(tc.tile_pool(name="wprep", bufs=2))
+        xs = stack.enter_context(tc.tile_pool(name="xs", bufs=N_GROUPS))
+        small = stack.enter_context(tc.tile_pool(name="small", bufs=6))
+        work = stack.enter_context(tc.tile_pool(name="work", bufs=4))
+        banks_t = stack.enter_context(tc.psum_pool(name="banks_t", bufs=2))
+        banks_acc = stack.enter_context(tc.psum_pool(name="banks_acc", bufs=4))
+
+        x_of, mean_var_of, neg_mean_of, rstd_of, xhat_of, grouped_of = {}, {}, {}, {}, {}, {}
+        w_rows_of, w_grouped_of = {}, {}
+
+        def load_group(g):
+            x = xs.tile([P, SLOTS, D], BF16, name="x")
+            nc.sync.dma_start(
+                out=x[:].rearrange("p j d -> p (j d)"),
+                in_=x_groups[g // GROUPS_PER_STREAM][g % GROUPS_PER_STREAM],
+            )
+            x_of[g] = x
+
+        for g in range(FIRST_LOADS):
+            load_group(g)
+
+        ident_f32 = const.tile([P, P], F32, name="ident_f32")
+        make_identity(nc, ident_f32[:])
+        ident_bf16 = const.tile([P, P], BF16, name="ident_bf16")
+        make_identity(nc, ident_bf16[:])
+        eps = const.tile([P, 1], F32, name="eps")
+        nc.vector.memset(eps[:], EPS)
+
+        ln_rows = const.tile([P, D], BF16, name="ln_rows")
+        nc.vector.memset(ln_rows[:], 0.0)
+        for v, vector in enumerate(ln_vectors):
+            nc.sync.dma_start(out=ln_rows[v : v + 1, :], in_=vector.rearrange("(o k) -> o k", o=1))
+        ln_rows_t = banks_acc.tile([P, PACK, P], BF16, name="ln_rows_t", tag="acc")
+        for t in range(PACK):
+            nc.tensor.transpose(
+                out=ln_rows_t[:, t, :], in_=ln_rows[:, t : D : PACK], identity=ident_bf16[:]
+            )
+        ln_cols = const.tile([P, PACK, len(ln_vectors)], F32, name="ln_cols")
+        nc.scalar.copy(out=ln_cols[:], in_=ln_rows_t[:, :, 0 : len(ln_vectors)])
+
+        bias_rows = const.tile([P, N_WEIGHTS * E], BF16, name="bias_rows")
+        nc.vector.memset(bias_rows[:], 0.0)
+        for w, bias in enumerate(biases):
+            nc.sync.dma_start(
+                out=bias_rows[0:1, w * E : (w + 1) * E], in_=bias.rearrange("(o e) -> o e", o=1)
+            )
+        ones = const.tile([P, P], BF16, name="ones")
+        nc.vector.memset(ones[:], 1.0)
+        bias_all = const.tile([P, N_WEIGHTS * E], F32, name="bias_all")
+        for c0 in range(0, N_WEIGHTS * E, BANK):
+            width = min(BANK, N_WEIGHTS * E - c0)
+            spread = banks_acc.tile([P, BANK], F32, name="spread", tag="acc")
+            nc.tensor.matmul(
+                out=spread[:, 0:width], lhsT=ones[:], rhs=bias_rows[:, c0 : c0 + width],
+                start=True, stop=True,
+            )
+            nc.scalar.copy(out=bias_all[:, c0 : c0 + width], in_=spread[:, 0:width])
+
+        w_codes = const.tile([P, N_WEIGHTS * E], U32, name="w_codes", align_bytes=64)
+        w_scales = const.tile([P, N_WEIGHTS * E], U8, name="w_scales", align_bytes=64)
+
+        def load_weight(w):
+            w_rows = wprep.tile([P, E // P, D], BF16, name="w_rows", bufs=N_WEIGHTS)
+            nc.sync.dma_start(out=w_rows[:], in_=weights[w].rearrange("(c p) k -> p c k", p=P))
+            w_rows_of[w] = w_rows
+
+        def transpose_weight(w):
+            w_grouped = wprep.tile([P, E, PACK], BF16, name="w_grouped", align_bytes=64)
+            for c in range(E // P):
+                w_t = banks_acc.tile([P, PACK, P], BF16, name="w_t", tag="acc")
+                for t in range(PACK):
+                    nc.tensor.transpose(
+                        out=w_t[:, t, :], in_=w_rows_of[w][:, c, t : D : PACK],
+                        identity=ident_bf16[:],
+                    )
+                nc.scalar.copy(
+                    out=w_grouped[:, c * P : (c + 1) * P, :], in_=w_t[:].rearrange("p t e -> p e t")
+                )
+            w_grouped_of[w] = w_grouped
+
+        def quantise_weight(w):
+            nc.vector.quantize_mx(
+                out=w_codes[:, w * E : (w + 1) * E].bitcast(FP8X4),
+                scales=w_scales[:, w * E : (w + 1) * E],
+                in_=w_grouped_of[w][:].rearrange("p e t -> p (e t)"),
+            )
+
+        def statistics(g):
+            halves = small.tile([P, SLOTS, 6], F32, name="halves")
+            mean_var = small.tile([P, SLOTS, 2], F32, name="mean_var")
+            for j in range(SLOTS):
+                nc.vector.bn_stats(out=halves[:, j, :], in_=x_of[g][:, j, :])
+            for j in range(SLOTS):
+                nc.vector.bn_aggr(out=mean_var[:, j, :], in_=halves[:, j, :])
+            mean_var_of[g] = mean_var
+
+        def standard_deviation(g):
+            std = small.tile([P, SLOTS], F32, name="std")
+            nc.scalar.activation(
+                out=std[:], in_=mean_var_of[g][:, :, 1], func=ACT.Sqrt, bias=eps[:, 0:1], scale=1.0
+            )
+            return std
+
+        def invert(g, std):
+            rstd = small.tile([P, SLOTS], F32, name="rstd")
+            nc.vector.reciprocal(out=rstd[:], in_=std[:])
+            rstd_of[g] = rstd
+
+        def negate_mean(g):
+            neg_mean = small.tile([P, SLOTS], F32, name="neg_mean")
+            nc.gpsimd.tensor_scalar(
+                out=neg_mean[:], in0=mean_var_of[g][:, :, 0], scalar1=-1.0, scalar2=0.0,
+                op0=ALU.mult, op1=ALU.add,
+            )
+            neg_mean_of[g] = neg_mean
+
+        def normalise(g):
+            xhat = work.tile([P, SLOTS, D], F32, name="xhat")
+            for j in range(SLOTS):
+                nc.gpsimd.tensor_scalar(
+                    out=xhat[:, j, :].rearrange("p (t q) -> p t q", t=PACK),
+                    in0=x_of[g][:, j, :].rearrange("p (q t) -> p t q", t=PACK),
+                    scalar1=neg_mean_of[g][:, j : j + 1], scalar2=rstd_of[g][:, j : j + 1],
+                    op0=ALU.add, op1=ALU.mult,
+                )
+            xhat_of[g] = xhat
+
+        def transpose_group(g):
+            xhat_t = []
+            for t0 in range(0, PACK, 2):
+                two_banks = banks_t.tile([P, 2, GROUP], F32, name="two_banks")
+                for t in range(t0, t0 + 2):
+                    for j in range(SLOTS):
+                        nc.tensor.transpose(
+                            out=two_banks[:, t - t0, j * P : (j + 1) * P],
+                            in_=xhat_of[g][:, j, t * P : (t + 1) * P],
+                            identity=ident_f32[:],
+                        )
+                    xhat_t.append(two_banks[:, t - t0, :])
+            return xhat_t
+
+        def gain_shift_group(g, xhat_t):
+            gain = 2 * (g // GROUPS_PER_STREAM)
+            planes = work.tile([P, PACK, GROUP], BF16, name="planes")
+            for t in range(PACK):
+                nc.scalar.activation(
+                    out=planes[:, t, :], in_=xhat_t[t], func=ACT.Identity,
+                    scale=ln_cols[:, t, gain : gain + 1], bias=ln_cols[:, t, gain + 1 : gain + 2],
+                )
+            grouped = work.tile([P, GROUP, PACK], BF16, name="grouped", align_bytes=64)
+            nc.scalar.copy(
+                out=grouped[:].rearrange("p (c i) t -> p c t i", i=4),
+                in_=planes[:].rearrange("p t (c i) -> p c t i", i=4),
+            )
+            grouped_of[g] = grouped
+
+        def quantise_group(g):
+            codes = work.tile([P, GROUP], U32, name="codes", align_bytes=64)
+            scales = work.tile([P, GROUP], U8, name="scales", align_bytes=64)
+            nc.vector.quantize_mx(
+                out=codes[:].bitcast(FP8X4), scales=scales[:],
+                in_=grouped_of[g][:].rearrange("p c t -> p (c t)"),
+            )
+            return codes, scales
+
+        def project_group(g, codes, scales):
+            result = work.tile([P, 3, SLOTS, E], F32, name="result")
+            for j0 in range(0, SLOTS, 2):
+                for o in range(3):
+                    w_cols = weight_columns(g, o)
+                    bias_twice = bias_all[:, w_cols].unsqueeze(1).to_broadcast([P, 2, E])
+                    last_bank = o == 2 and j0 == SLOTS - 2
+                    acc = banks_acc.tile([P, 2, E], F32, name="acc", tag="acc")
+                    for jj in range(2):
+                        tokens = slice((j0 + jj) * P, (j0 + jj + 1) * P)
+                        nc.tensor.matmul_mx(
+                            out=acc[:, jj, :],
+                            lhsT=codes[:, tokens].bitcast(FP8X4), lhsT_scale=scales[:, tokens],
+                            rhs=w_codes[:, w_cols].bitcast(FP8X4), rhs_scale=w_scales[:, w_cols],
+                            start=True, stop=True,
+                        )
+                    two_slots = result[:, o, j0 : j0 + 2, :]
+                    if last_bank:
+                        nc.scalar.copy(out=two_slots, in_=acc[:])
+                        nc.gpsimd.tensor_tensor(
+                            out=two_slots, in0=two_slots, in1=bias_twice, op=ALU.add
+                        )
+                    else:
+                        nc.vector.tensor_tensor(out=two_slots, in0=acc[:], in1=bias_twice, op=ALU.add)
+            for o in range(3):
+                nc.sync.dma_start(
+                    out=out_groups[o][g], in_=result[:, o, :, :].rearrange("p j e -> p (j e)")
+                )
+
+        def in_range(g):
+            return 0 <= g < N_GROUPS
+
+        for w in range(N_WEIGHTS):
+            load_weight(w)
+        for g in range(FIRST_LOADS, N_GROUPS):
+            load_group(g)
+
+        for i in range(N_GROUPS + LAG_PROJECT):
+            if in_range(i - LAG_PROJECT):
+                codes, scales = quantise_group(i - LAG_PROJECT)
+            if in_range(i - LAG_TRANSPOSE):
+                xhat_t = transpose_group(i - LAG_TRANSPOSE)
+            if 0 <= i - 1 < N_WEIGHTS:
+                transpose_weight(i - 1)
+            if in_range(i - LAG_SCALARS):
+                std = standard_deviation(i - LAG_SCALARS)
+                negate_mean(i - LAG_SCALARS)
+            if in_range(i - LAG_NORMALISE):
+                normalise(i - LAG_NORMALISE)
+            if in_range(i - LAG_TRANSPOSE):
+                gain_shift_group(i - LAG_TRANSPOSE, xhat_t)
+            if in_range(i):
+                statistics(i)
+            if in_range(i - LAG_SCALARS):
+                invert(i - LAG_SCALARS, std)
+            if 0 <= i - 1 < N_WEIGHTS:
+                quantise_weight(i - 1)
+            if in_range(i - LAG_PROJECT):
+                project_group(i - LAG_PROJECT, codes, scales)

@@ -14,6 +14,7 @@ ALU = mybir.AluOpType
 P = 128
 PACK = 4
 D = P * PACK
+WORDS = D // 2
 E = 256
 SLOTS = 4
 GROUP = P * SLOTS
@@ -125,17 +126,20 @@ def tile_modalityadaptivemodule_pa_t_kernel(
             w_rows_of[w] = w_rows
 
         def transpose_weight(w):
-            w_grouped = wprep.tile([P, E, PACK], BF16, name="w_grouped", align_bytes=64)
+            words = w_rows_of[w][:].rearrange("p c k -> p (c k)").bitcast(F32)
+            w_t = banks_acc.tile([P, 2, E], F32, name="w_t", tag="acc")
             for c in range(E // P):
-                w_t = banks_acc.tile([P, PACK, P], BF16, name="w_t", tag="acc")
-                for t in range(PACK):
+                for u in range(2):
                     nc.tensor.transpose(
-                        out=w_t[:, t, :], in_=w_rows_of[w][:, c, t : D : PACK],
-                        identity=ident_bf16[:],
+                        out=w_t[:, u, c * P : (c + 1) * P],
+                        in_=words[:, c * WORDS + u : (c + 1) * WORDS : 2], identity=ident_f32[:],
                     )
-                nc.scalar.copy(
-                    out=w_grouped[:, c * P : (c + 1) * P, :], in_=w_t[:].rearrange("p t e -> p e t")
-                )
+            w_grouped = wprep.tile([P, E, PACK], BF16, name="w_grouped", align_bytes=64)
+            grouped_words = w_grouped[:].rearrange("p e t -> p (e t)").bitcast(F32)
+            nc.scalar.copy(
+                out=grouped_words.rearrange("p (e u) -> p e u", u=2),
+                in_=w_t[:].rearrange("p u e -> p e u"),
+            )
             w_grouped_of[w] = w_grouped
 
         def quantise_weight(w):
@@ -154,23 +158,16 @@ def tile_modalityadaptivemodule_pa_t_kernel(
                 nc.vector.bn_aggr(out=mean_var[:, j, :], in_=halves[:, j, :])
             mean_var_of[g] = mean_var
 
-        def standard_deviation(g):
-            std = small.tile([P, SLOTS], F32, name="std")
-            nc.scalar.activation(
-                out=std[:], in_=mean_var_of[g][:, :, 1], func=ACT.Sqrt, bias=eps[:, 0:1], scale=1.0
-            )
-            return std
-
-        def invert(g, std):
+        def token_scalars(g):
             rstd = small.tile([P, SLOTS], F32, name="rstd")
-            nc.vector.reciprocal(out=rstd[:], in_=std[:])
+            nc.scalar.activation(
+                out=rstd[:], in_=mean_var_of[g][:, :, 1], func=ACT.Abs_reciprocal_sqrt,
+                bias=eps[:, 0:1], scale=1.0,
+            )
             rstd_of[g] = rstd
-
-        def negate_mean(g):
             neg_mean = small.tile([P, SLOTS], F32, name="neg_mean")
-            nc.gpsimd.tensor_scalar(
-                out=neg_mean[:], in0=mean_var_of[g][:, :, 0], scalar1=-1.0, scalar2=0.0,
-                op0=ALU.mult, op1=ALU.add,
+            nc.scalar.activation(
+                out=neg_mean[:], in_=mean_var_of[g][:, :, 0], func=ACT.Copy, scale=-1.0
             )
             neg_mean_of[g] = neg_mean
 
@@ -268,16 +265,13 @@ def tile_modalityadaptivemodule_pa_t_kernel(
             if 0 <= i - 1 < N_WEIGHTS:
                 transpose_weight(i - 1)
             if in_range(i - LAG_SCALARS):
-                std = standard_deviation(i - LAG_SCALARS)
-                negate_mean(i - LAG_SCALARS)
+                token_scalars(i - LAG_SCALARS)
             if in_range(i - LAG_NORMALISE):
                 normalise(i - LAG_NORMALISE)
             if in_range(i - LAG_TRANSPOSE):
                 gain_shift_group(i - LAG_TRANSPOSE, xhat_t)
             if in_range(i):
                 statistics(i)
-            if in_range(i - LAG_SCALARS):
-                invert(i - LAG_SCALARS, std)
             if 0 <= i - 1 < N_WEIGHTS:
                 quantise_weight(i - 1)
             if in_range(i - LAG_PROJECT):

@@ -136,10 +136,12 @@ def tile_modalityadaptivemodule_pa_t_kernel(
                     )
             w_grouped = wprep.tile([P, E, PACK], BF16, name="w_grouped", align_bytes=64)
             grouped_words = w_grouped[:].rearrange("p e t -> p (e t)").bitcast(F32)
-            nc.scalar.copy(
-                out=grouped_words.rearrange("p (e u) -> p e u", u=2),
-                in_=w_t[:].rearrange("p u e -> p e u"),
-            )
+            out = grouped_words.rearrange("p (e u) -> p e u", u=2)
+            in_ = w_t[:].rearrange("p u e -> p e u")
+            if w == 0:
+                nc.vector.tensor_copy(out=out, in_=in_)
+            else:
+                nc.scalar.copy(out=out, in_=in_)
             w_grouped_of[w] = w_grouped
 
         def quantise_weight(w):
@@ -173,13 +175,22 @@ def tile_modalityadaptivemodule_pa_t_kernel(
 
         def normalise(g):
             xhat = work.tile([P, SLOTS, D], F32, name="xhat")
+            by_scalar = g % 2 if g > 1 else 0
             for j in range(SLOTS):
-                nc.gpsimd.tensor_scalar(
-                    out=xhat[:, j, :].rearrange("p (t q) -> p t q", t=PACK),
-                    in0=x_of[g][:, j, :].rearrange("p (q t) -> p t q", t=PACK),
-                    scalar1=neg_mean_of[g][:, j : j + 1], scalar2=rstd_of[g][:, j : j + 1],
-                    op0=ALU.add, op1=ALU.mult,
-                )
+                out = xhat[:, j, :].rearrange("p (t q) -> p t q", t=PACK)
+                in_ = x_of[g][:, j, :].rearrange("p (q t) -> p t q", t=PACK)
+                neg_mean = neg_mean_of[g][:, j : j + 1]
+                rstd = rstd_of[g][:, j : j + 1]
+                if j < SLOTS - by_scalar:
+                    nc.gpsimd.tensor_scalar(
+                        out=out, in0=in_, scalar1=neg_mean, scalar2=rstd, op0=ALU.add, op1=ALU.mult
+                    )
+                else:
+                    offset = small.tile([P, 1], F32, name="offset")
+                    nc.scalar.activation(out=offset[:], in_=neg_mean, func=ACT.Copy, scale=rstd)
+                    nc.scalar.activation(
+                        out=out, in_=in_, func=ACT.Identity, scale=rstd, bias=offset[:, 0:1]
+                    )
             xhat_of[g] = xhat
 
         def transpose_group(g):

@@ -27,11 +27,16 @@ EPS = 1e-5
 
 FLOPS = 2 * (2 * TOKENS) * D * (3 * E)
 
-FIRST_LOADS = 2
+LATE = 12
+FIRST_WEIGHTS = 3
 LAG_SCALARS = 1
 LAG_NORMALISE = 2
 LAG_TRANSPOSE = 3
 LAG_PROJECT = 5
+
+
+def scalar_slots(g):
+    return (0, 2) if g in range(3, LATE, 2) or g == N_GROUPS - 1 else (2,)
 
 
 def tile_modalityadaptivemodule_pa_t_kernel(
@@ -77,8 +82,14 @@ def tile_modalityadaptivemodule_pa_t_kernel(
             )
             x_of[g] = x
 
-        for g in range(FIRST_LOADS):
-            load_group(g)
+        def load_weight(w):
+            w_rows = wprep.tile([P, E // P, D], BF16, name="w_rows", bufs=N_WEIGHTS)
+            nc.sync.dma_start(out=w_rows[:], in_=weights[w].rearrange("(c p) k -> p c k", p=P))
+            w_rows_of[w] = w_rows
+
+        load_group(0)
+        for w in range(FIRST_WEIGHTS):
+            load_weight(w)
 
         ident_f32 = const.tile([P, P], F32, name="ident_f32")
         make_identity(nc, ident_f32[:])
@@ -108,22 +119,19 @@ def tile_modalityadaptivemodule_pa_t_kernel(
         ones = const.tile([P, P], BF16, name="ones")
         nc.vector.memset(ones[:], 1.0)
         bias_all = const.tile([P, N_WEIGHTS * E], F32, name="bias_all")
-        for c0 in range(0, N_WEIGHTS * E, BANK):
-            width = min(BANK, N_WEIGHTS * E - c0)
-            spread = banks_acc.tile([P, BANK], F32, name="spread", tag="acc")
-            nc.tensor.matmul(
-                out=spread[:, 0:width], lhsT=ones[:], rhs=bias_rows[:, c0 : c0 + width],
-                start=True, stop=True,
-            )
-            nc.scalar.copy(out=bias_all[:, c0 : c0 + width], in_=spread[:, 0:width])
+
+        def spread_biases():
+            for c0 in range(0, N_WEIGHTS * E, BANK):
+                width = min(BANK, N_WEIGHTS * E - c0)
+                spread = banks_acc.tile([P, BANK], F32, name="spread", tag="acc")
+                nc.tensor.matmul(
+                    out=spread[:, 0:width], lhsT=ones[:], rhs=bias_rows[:, c0 : c0 + width],
+                    start=True, stop=True,
+                )
+                nc.scalar.copy(out=bias_all[:, c0 : c0 + width], in_=spread[:, 0:width])
 
         w_codes = const.tile([P, N_WEIGHTS * E], U32, name="w_codes", align_bytes=64)
         w_scales = const.tile([P, N_WEIGHTS * E], U8, name="w_scales", align_bytes=64)
-
-        def load_weight(w):
-            w_rows = wprep.tile([P, E // P, D], BF16, name="w_rows", bufs=N_WEIGHTS)
-            nc.sync.dma_start(out=w_rows[:], in_=weights[w].rearrange("(c p) k -> p c k", p=P))
-            w_rows_of[w] = w_rows
 
         def transpose_weight(w):
             words = w_rows_of[w][:].rearrange("p c k -> p (c k)").bitcast(F32)
@@ -134,14 +142,11 @@ def tile_modalityadaptivemodule_pa_t_kernel(
                         out=w_t[:, u, c * P : (c + 1) * P],
                         in_=words[:, c * WORDS + u : (c + 1) * WORDS : 2], identity=ident_f32[:],
                     )
-            w_grouped = wprep.tile([P, E, PACK], BF16, name="w_grouped", align_bytes=64)
+            w_grouped = wprep.tile([P, E, PACK], BF16, name="w_grouped", bufs=FIRST_WEIGHTS, align_bytes=64)
             grouped_words = w_grouped[:].rearrange("p e t -> p (e t)").bitcast(F32)
             out = grouped_words.rearrange("p (e u) -> p e u", u=2)
             in_ = w_t[:].rearrange("p u e -> p e u")
-            if w == 0:
-                nc.vector.tensor_copy(out=out, in_=in_)
-            else:
-                nc.scalar.copy(out=out, in_=in_)
+            nc.scalar.copy(out=out, in_=in_)
             w_grouped_of[w] = w_grouped
 
         def quantise_weight(w):
@@ -175,7 +180,7 @@ def tile_modalityadaptivemodule_pa_t_kernel(
 
         def normalise(g):
             xhat = work.tile([P, SLOTS, D], F32, name="xhat")
-            by_scalar = g % 2 if g > 1 else 0
+            by_scalar = 1 if g in range(2, LATE, 2) else 0
             for j in range(SLOTS):
                 out = xhat[:, j, :].rearrange("p (t q) -> p t q", t=PACK)
                 in_ = x_of[g][:, j, :].rearrange("p (q t) -> p t q", t=PACK)
@@ -237,7 +242,7 @@ def tile_modalityadaptivemodule_pa_t_kernel(
                 for o in range(3):
                     w_cols = weight_columns(g, o)
                     bias_twice = bias_all[:, w_cols].unsqueeze(1).to_broadcast([P, 2, E])
-                    last_bank = o == 2 and j0 == SLOTS - 2
+                    by_scalar = o == 2 and j0 in scalar_slots(g)
                     acc = banks_acc.tile([P, 2, E], F32, name="acc", tag="acc")
                     for jj in range(2):
                         tokens = slice((j0 + jj) * P, (j0 + jj + 1) * P)
@@ -248,7 +253,7 @@ def tile_modalityadaptivemodule_pa_t_kernel(
                             start=True, stop=True,
                         )
                     two_slots = result[:, o, j0 : j0 + 2, :]
-                    if last_bank:
+                    if by_scalar:
                         nc.scalar.copy(out=two_slots, in_=acc[:])
                         nc.gpsimd.tensor_tensor(
                             out=two_slots, in0=two_slots, in1=bias_twice, op=ALU.add
@@ -263,18 +268,27 @@ def tile_modalityadaptivemodule_pa_t_kernel(
         def in_range(g):
             return 0 <= g < N_GROUPS
 
-        for w in range(N_WEIGHTS):
-            load_weight(w)
-        for g in range(FIRST_LOADS, N_GROUPS):
+        for g in range(1, 4):
             load_group(g)
+        for w in range(FIRST_WEIGHTS, N_WEIGHTS):
+            load_weight(w)
+        for g in range(4, N_GROUPS):
+            load_group(g)
+
+        def weights_in_turn(i):
+            if i == 1:
+                return range(FIRST_WEIGHTS)
+            return [i - 1] if FIRST_WEIGHTS <= i - 1 < N_WEIGHTS else []
 
         for i in range(N_GROUPS + LAG_PROJECT):
             if in_range(i - LAG_PROJECT):
                 codes, scales = quantise_group(i - LAG_PROJECT)
             if in_range(i - LAG_TRANSPOSE):
                 xhat_t = transpose_group(i - LAG_TRANSPOSE)
-            if 0 <= i - 1 < N_WEIGHTS:
-                transpose_weight(i - 1)
+            for w in weights_in_turn(i):
+                transpose_weight(w)
+            if i == 1:
+                spread_biases()
             if in_range(i - LAG_SCALARS):
                 token_scalars(i - LAG_SCALARS)
             if in_range(i - LAG_NORMALISE):
@@ -283,7 +297,7 @@ def tile_modalityadaptivemodule_pa_t_kernel(
                 gain_shift_group(i - LAG_TRANSPOSE, xhat_t)
             if in_range(i):
                 statistics(i)
-            if 0 <= i - 1 < N_WEIGHTS:
-                quantise_weight(i - 1)
+            for w in weights_in_turn(i):
+                quantise_weight(w)
             if in_range(i - LAG_PROJECT):
                 project_group(i - LAG_PROJECT, codes, scales)

from contextlib import ExitStack

import concourse.mybir as mybir
from concourse.masks import make_identity

F32 = mybir.dt.float32
BF16 = mybir.dt.bfloat16
U32 = mybir.dt.uint32
U8 = mybir.dt.uint8
FP8X4 = mybir.dt.float8_e4m3fn_x4
ACT = mybir.ActivationFunctionType
ALU = mybir.AluOpType

P = 128
PACK = 4
D = P * PACK
WORDS = D // 2
E = 256
SLOTS = 4
GROUP = P * SLOTS
TOKENS = 4096
GROUPS_PER_STREAM = TOKENS // GROUP
N_GROUPS = 2 * GROUPS_PER_STREAM
N_WEIGHTS = 5
BANK = 512
EPS = 1e-5

FLOPS = 2 * (2 * TOKENS) * D * (3 * E)

LATE = 12
FIRST_WEIGHTS = 3
LAG_SCALARS = 1
LAG_NORMALISE = 2
LAG_TRANSPOSE = 3
LAG_PROJECT = 5


def scalar_slots(g):
    return (0, 2) if g in range(3, LATE, 2) or g == N_GROUPS - 1 else (2,)


def tile_modalityadaptivemodule_pa_t_kernel(
    tc,
    text, img, ln_t_g, ln_t_b, ln_i_g, ln_i_b,
    Wq, bq, Wkt, bkt, Wvt, bvt, Wki, bki, Wvi, bvi,
    out_0, out_1, out_2,
):
    nc = tc.nc
    weights = [Wq, Wkt, Wvt, Wki, Wvi]
    biases = [bq, bkt, bvt, bki, bvi]
    ln_vectors = [ln_t_g, ln_t_b, ln_i_g, ln_i_b]

    def weight_columns(g, o):
        w = 0 if o == 0 else o + 2 * (g // GROUPS_PER_STREAM)
        return slice(w * E, (w + 1) * E)

    x_groups = [
        s.flatten_outer_dims().rearrange("(g p j) d -> g p (j d)", p=P, j=SLOTS) for s in (text, img)
    ]
    out_groups = [
        o.flatten_outer_dims().rearrange("(g p j) e -> g p (j e)", p=P, j=SLOTS)
        for o in (out_0, out_1, out_2)
    ]

    with ExitStack() as stack:
        const = stack.enter_context(tc.tile_pool(name="const", bufs=1))
        wprep = stack.enter_context(tc.tile_pool(name="wprep", bufs=2))
        xs = stack.enter_context(tc.tile_pool(name="xs", bufs=N_GROUPS))
        small = stack.enter_context(tc.tile_pool(name="small", bufs=6))
        work = stack.enter_context(tc.tile_pool(name="work", bufs=4))
        banks_t = stack.enter_context(tc.psum_pool(name="banks_t", bufs=2))
        banks_acc = stack.enter_context(tc.psum_pool(name="banks_acc", bufs=4))

        x_of, mean_var_of, neg_mean_of, rstd_of, xhat_of, grouped_of = {}, {}, {}, {}, {}, {}
        w_rows_of, w_grouped_of = {}, {}

        def load_group(g):
            x = xs.tile([P, SLOTS, D], BF16, name="x")
            nc.sync.dma_start(
                out=x[:].rearrange("p j d -> p (j d)"),
                in_=x_groups[g // GROUPS_PER_STREAM][g % GROUPS_PER_STREAM],
            )
            x_of[g] = x

        def load_weight(w):
            w_rows = wprep.tile([P, E // P, D], BF16, name="w_rows", bufs=N_WEIGHTS)
            nc.sync.dma_start(out=w_rows[:], in_=weights[w].rearrange("(c p) k -> p c k", p=P))
            w_rows_of[w] = w_rows

        load_group(0)
        for w in range(FIRST_WEIGHTS):
            load_weight(w)

        ident_f32 = const.tile([P, P], F32, name="ident_f32")
        make_identity(nc, ident_f32[:])
        ident_bf16 = const.tile([P, P], BF16, name="ident_bf16")
        make_identity(nc, ident_bf16[:])
        eps = const.tile([P, 1], F32, name="eps")
        nc.vector.memset(eps[:], EPS)

        ln_rows = const.tile([P, D], BF16, name="ln_rows")
        nc.vector.memset(ln_rows[:], 0.0)
        for v, vector in enumerate(ln_vectors):
            nc.sync.dma_start(out=ln_rows[v : v + 1, :], in_=vector.rearrange("(o k) -> o k", o=1))
        ln_rows_t = banks_acc.tile([P, PACK, P], BF16, name="ln_rows_t", tag="acc")
        for t in range(PACK):
            nc.tensor.transpose(
                out=ln_rows_t[:, t, :], in_=ln_rows[:, t : D : PACK], identity=ident_bf16[:]
            )
        ln_cols = const.tile([P, PACK, len(ln_vectors)], F32, name="ln_cols")
        nc.scalar.copy(out=ln_cols[:], in_=ln_rows_t[:, :, 0 : len(ln_vectors)])

        bias_rows = const.tile([P, N_WEIGHTS * E], BF16, name="bias_rows")
        nc.vector.memset(bias_rows[:], 0.0)
        for w, bias in enumerate(biases):
            nc.sync.dma_start(
                out=bias_rows[0:1, w * E : (w + 1) * E], in_=bias.rearrange("(o e) -> o e", o=1)
            )
        ones = const.tile([P, P], BF16, name="ones")
        nc.vector.memset(ones[:], 1.0)
        bias_all = const.tile([P, N_WEIGHTS * E], F32, name="bias_all")

        def spread_biases():
            for c0 in range(0, N_WEIGHTS * E, BANK):
                width = min(BANK, N_WEIGHTS * E - c0)
                spread = banks_acc.tile([P, BANK], F32, name="spread", tag="acc")
                nc.tensor.matmul(
                    out=spread[:, 0:width], lhsT=ones[:], rhs=bias_rows[:, c0 : c0 + width],
                    start=True, stop=True,
                )
                nc.scalar.copy(out=bias_all[:, c0 : c0 + width], in_=spread[:, 0:width])

        w_codes = const.tile([P, N_WEIGHTS * E], U32, name="w_codes", align_bytes=64)
        w_scales = const.tile([P, N_WEIGHTS * E], U8, name="w_scales", align_bytes=64)

        def transpose_weight(w):
            words = w_rows_of[w][:].rearrange("p c k -> p (c k)").bitcast(F32)
            w_t = banks_acc.tile([P, 2, E], F32, name="w_t", tag="acc")
            for c in range(E // P):
                for u in range(2):
                    nc.tensor.transpose(
                        out=w_t[:, u, c * P : (c + 1) * P],
                        in_=words[:, c * WORDS + u : (c + 1) * WORDS : 2], identity=ident_f32[:],
                    )
            w_grouped = wprep.tile([P, E, PACK], BF16, name="w_grouped", bufs=FIRST_WEIGHTS, align_bytes=64)
            grouped_words = w_grouped[:].rearrange("p e t -> p (e t)").bitcast(F32)
            out = grouped_words.rearrange("p (e u) -> p e u", u=2)
            in_ = w_t[:].rearrange("p u e -> p e u")
            nc.scalar.copy(out=out, in_=in_)
            w_grouped_of[w] = w_grouped

        def quantise_weight(w):
            nc.vector.quantize_mx(
                out=w_codes[:, w * E : (w + 1) * E].bitcast(FP8X4),
                scales=w_scales[:, w * E : (w + 1) * E],
                in_=w_grouped_of[w][:].rearrange("p e t -> p (e t)"),
            )

        def statistics(g):
            halves = small.tile([P, SLOTS, 6], F32, name="halves")
            mean_var = small.tile([P, SLOTS, 2], F32, name="mean_var")
            for j in range(SLOTS):
                nc.vector.bn_stats(out=halves[:, j, :], in_=x_of[g][:, j, :])
            for j in range(SLOTS):
                nc.vector.bn_aggr(out=mean_var[:, j, :], in_=halves[:, j, :])
            mean_var_of[g] = mean_var

        def token_scalars(g):
            rstd = small.tile([P, SLOTS], F32, name="rstd")
            nc.scalar.activation(
                out=rstd[:], in_=mean_var_of[g][:, :, 1], func=ACT.Abs_reciprocal_sqrt,
                bias=eps[:, 0:1], scale=1.0,
            )
            rstd_of[g] = rstd
            neg_mean = small.tile([P, SLOTS], F32, name="neg_mean")
            nc.scalar.activation(
                out=neg_mean[:], in_=mean_var_of[g][:, :, 0], func=ACT.Copy, scale=-1.0
            )
            neg_mean_of[g] = neg_mean

        def normalise(g):
            xhat = work.tile([P, SLOTS, D], F32, name="xhat")
            by_scalar = 1 if g in range(2, LATE, 2) else 0
            for j in range(SLOTS):
                out = xhat[:, j, :].rearrange("p (t q) -> p t q", t=PACK)
                in_ = x_of[g][:, j, :].rearrange("p (q t) -> p t q", t=PACK)
                neg_mean = neg_mean_of[g][:, j : j + 1]
                rstd = rstd_of[g][:, j : j + 1]
                if j < SLOTS - by_scalar:
                    nc.gpsimd.tensor_scalar(
                        out=out, in0=in_, scalar1=neg_mean, scalar2=rstd, op0=ALU.add, op1=ALU.mult
                    )
                else:
                    offset = small.tile([P, 1], F32, name="offset")
                    nc.scalar.activation(out=offset[:], in_=neg_mean, func=ACT.Copy, scale=rstd)
                    nc.scalar.activation(
                        out=out, in_=in_, func=ACT.Identity, scale=rstd, bias=offset[:, 0:1]
                    )
            xhat_of[g] = xhat

        def transpose_group(g):
            xhat_t = []
            for t0 in range(0, PACK, 2):
                two_banks = banks_t.tile([P, 2, GROUP], F32, name="two_banks")
                for t in range(t0, t0 + 2):
                    for j in range(SLOTS):
                        nc.tensor.transpose(
                            out=two_banks[:, t - t0, j * P : (j + 1) * P],
                            in_=xhat_of[g][:, j, t * P : (t + 1) * P],
                            identity=ident_f32[:],
                        )
                    xhat_t.append(two_banks[:, t - t0, :])
            return xhat_t

        def gain_shift_group(g, xhat_t):
            gain = 2 * (g // GROUPS_PER_STREAM)
            planes = work.tile([P, PACK, GROUP], BF16, name="planes")
            for t in range(PACK):
                nc.scalar.activation(
                    out=planes[:, t, :], in_=xhat_t[t], func=ACT.Identity,
                    scale=ln_cols[:, t, gain : gain + 1], bias=ln_cols[:, t, gain + 1 : gain + 2],
                )
            grouped = work.tile([P, GROUP, PACK], BF16, name="grouped", align_bytes=64)
            nc.scalar.copy(
                out=grouped[:].rearrange("p (c i) t -> p c t i", i=4),
                in_=planes[:].rearrange("p t (c i) -> p c t i", i=4),
            )
            grouped_of[g] = grouped

        def quantise_group(g):
            codes = work.tile([P, GROUP], U32, name="codes", align_bytes=64)
            scales = work.tile([P, GROUP], U8, name="scales", align_bytes=64)
            nc.vector.quantize_mx(
                out=codes[:].bitcast(FP8X4), scales=scales[:],
                in_=grouped_of[g][:].rearrange("p c t -> p (c t)"),
            )
            return codes, scales

        def project_group(g, codes, scales):
            result = work.tile([P, 3, SLOTS, E], F32, name="result")
            for j0 in range(0, SLOTS, 2):
                for o in range(3):
                    w_cols = weight_columns(g, o)
                    bias_twice = bias_all[:, w_cols].unsqueeze(1).to_broadcast([P, 2, E])
                    by_scalar = o == 2 and j0 in scalar_slots(g)
                    acc = banks_acc.tile([P, 2, E], F32, name="acc", tag="acc")
                    for jj in range(2):
                        tokens = slice((j0 + jj) * P, (j0 + jj + 1) * P)
                        nc.tensor.matmul_mx(
                            out=acc[:, jj, :],
                            lhsT=codes[:, tokens].bitcast(FP8X4), lhsT_scale=scales[:, tokens],
                            rhs=w_codes[:, w_cols].bitcast(FP8X4), rhs_scale=w_scales[:, w_cols],
                            start=True, stop=True,
                        )
                    two_slots = result[:, o, j0 : j0 + 2, :]
                    if by_scalar:
                        nc.scalar.copy(out=two_slots, in_=acc[:])
                        nc.gpsimd.tensor_tensor(
                            out=two_slots, in0=two_slots, in1=bias_twice, op=ALU.add
                        )
                    else:
                        nc.vector.tensor_tensor(out=two_slots, in0=acc[:], in1=bias_twice, op=ALU.add)
            for o in range(3):
                nc.sync.dma_start(
                    out=out_groups[o][g], in_=result[:, o, :, :].rearrange("p j e -> p (j e)")
                )

        def in_range(g):
            return 0 <= g < N_GROUPS

        for g in range(1, 4):
            load_group(g)
        for w in range(FIRST_WEIGHTS, N_WEIGHTS):
            load_weight(w)
        for g in range(4, N_GROUPS):
            load_group(g)

        def weights_in_turn(i):
            if i == 1:
                return range(FIRST_WEIGHTS)
            return [i - 1] if FIRST_WEIGHTS <= i - 1 < N_WEIGHTS else []

        for i in range(N_GROUPS + LAG_PROJECT):
            if in_range(i - LAG_PROJECT):
                codes, scales = quantise_group(i - LAG_PROJECT)
            if in_range(i - LAG_TRANSPOSE):
                xhat_t = transpose_group(i - LAG_TRANSPOSE)
            for w in weights_in_turn(i):
                transpose_weight(w)
            if i == 1:
                spread_biases()
            if in_range(i - LAG_SCALARS):
                token_scalars(i - LAG_SCALARS)
            if in_range(i - LAG_NORMALISE):
                normalise(i - LAG_NORMALISE)
            if in_range(i - LAG_TRANSPOSE):
                gain_shift_group(i - LAG_TRANSPOSE, xhat_t)
            if in_range(i):
                statistics(i)
            for w in weights_in_turn(i):
                quantise_weight(w)
            if in_range(i - LAG_PROJECT):
                project_group(i - LAG_PROJECT, codes, scales)
